import numpy as np
import ml_dtypes


def mxq(x, axis, fmt="e4m3"):
    dtype, down = {"e4m3": (ml_dtypes.float8_e4m3fn, 7), "e5m2": (ml_dtypes.float8_e5m2, 14)}[fmt]
    v = np.moveaxis(np.asarray(x, np.float32).astype(ml_dtypes.bfloat16).astype(np.float64), axis, -1)
    blocks = v.reshape(v.shape[:-1] + (-1, 32))
    amax = np.abs(blocks).max(-1, keepdims=True)
    byte = np.maximum(np.where(amax > 0, np.frexp(amax)[1] - 1 + 127, 0) - down, 1)
    scale = np.exp2(byte - 127.0)
    codes = (blocks / scale).astype(np.float32).astype(dtype).astype(np.float64)
    return np.moveaxis((codes * scale).reshape(v.shape), -1, axis)


WIDE = False


def mx_kscale(k):
    if not WIDE:
        return np.ones(k)
    levels = np.array([10, -10, 5, -5, 0])
    a = np.random.permutation(np.resize(levels, k // 512 * 4)).reshape(k // 512, 4)
    idx = np.arange(k)
    return np.exp2(a[idx // 512, idx % 128 // 32])


BF16 = ml_dtypes.bfloat16


def bf(x):
    return np.asarray(x, np.float32).astype(BF16)


def f64(x):
    return np.asarray(x).astype(np.float64)


B, N, G, L = 256, 4096, 128, 768
N2 = 2 * N
L2 = 2 * L
L_LIMIT = 1.0


def relu(v):
    return np.maximum(v, 0.0)


def setup_inputs():
    s, t = mx_kscale(N2), mx_kscale(L2)
    return {
        "Volt": bf(np.random.standard_normal((B, N2)) * s),
        "IM": bf(np.random.standard_normal((L2, N2)) / np.sqrt(N2) / s[None, :] * t[:, None]),
        "Ybr": bf(np.random.standard_normal((L2, L2)) / np.sqrt(L2) / t[None, :]),
        "n_o_mu_i_u": bf(np.random.standard_normal((B, L))),
    }


def reference(Volt, IM, Ybr, n_o_mu_i_u):
    mu = f64(n_o_mu_i_u)
    dv = mxq(f64(Volt), 1, "e4m3") @ mxq(f64(IM), 1, "e4m3").T
    Ibr = mxq(dv, 1, "e4m3") @ mxq(f64(Ybr), 1, "e4m3").T
    i_up = Ibr[:, :L] ** 2 + Ibr[:, L:] ** 2 - L_LIMIT ** 2
    out = np.sum(relu(i_up), axis=1)
    out = out + np.sum(np.abs(mu * i_up), axis=1)
    out = out + np.sum(relu(-mu), axis=1)
    return out

@@ -1,0 +1,228 @@
+from contextlib import ExitStack
+
+import concourse.mybir as mybir
+from concourse.masks import make_identity
+
+F32 = mybir.dt.float32
+BF16 = mybir.dt.bfloat16
+U32 = mybir.dt.uint32
+U8 = mybir.dt.uint8
+FP8X4 = mybir.dt.float8_e4m3fn_x4
+ALU = mybir.AluOpType
+ACT = mybir.ActivationFunctionType
+
+P = 128
+PACK = 4
+K_PASS = P * PACK
+
+SAMPLES = 256
+VOLTS = 8192
+CURRENTS = 1536
+LINES = CURRENTS // 2
+LIMIT_SQUARED = 1.0
+
+PASSES_1 = VOLTS // K_PASS
+PASSES_2 = CURRENTS // K_PASS
+SAMPLE_TILES = SAMPLES // P
+
+BANK_COLS = 2 * P
+CHUNK_BANKS = 4
+CHUNK_K = 4096
+IM_TILES = CURRENTS // P
+IM_CHUNKS = VOLTS // CHUNK_K
+VOLT_CHUNKS = SAMPLES * VOLTS // (P * CHUNK_K)
+YBR_UNITS = CURRENTS // BANK_COLS
+FIRST_YBR_STEP = IM_TILES - YBR_UNITS
+LINE_TILES = LINES // BANK_COLS
+
+FLOPS = 2 * SAMPLES * CURRENTS * (VOLTS + CURRENTS)
+
+
+def tile_pinnlayer_pa_k_kernel(tc, Volt, IM, Ybr, n_o_mu_i_u, out):
+    nc = tc.nc
+    with ExitStack() as ctx:
+        keep = ctx.enter_context(tc.tile_pool(name="keep", bufs=1))
+        raw_pool = ctx.enter_context(tc.tile_pool(name="raw", bufs=8))
+        grouped_pool = ctx.enter_context(tc.tile_pool(name="grouped", bufs=3))
+        im_pool = ctx.enter_context(tc.tile_pool(name="im", bufs=3))
+        work = ctx.enter_context(tc.tile_pool(name="work", bufs=3))
+        bank_pool = ctx.enter_context(tc.psum_pool(name="bank", bufs=6))
+        acc_pool = ctx.enter_context(tc.psum_pool(name="acc", bufs=2))
+        ctx.enter_context(tc.manual_schedule())
+
+        identity = keep.tile([P, P], F32)
+        make_identity(nc, identity[:])
+
+        terms = keep.tile([P, SAMPLE_TILES, 2, 8], F32)
+        nc.vector.memset(terms[:], 0.0)
+        totals = keep.tile([P, P], F32)
+        nc.vector.memset(totals[:], 0.0)
+        table_warmer = keep.tile([P, 1], F32)
+        nc.scalar.activation(out=table_warmer[:], in_=totals[:, 0:1], func=ACT.Abs)
+
+        volt_codes = keep.tile([P, PASSES_1, SAMPLES], U32, align_bytes=64)
+        volt_scales = keep.tile([P, PASSES_1, SAMPLES], U8, align_bytes=64)
+        ybr_codes = keep.tile([P, YBR_UNITS, PASSES_2, BANK_COLS], U32, align_bytes=64)
+        ybr_scales = keep.tile([P, YBR_UNITS, PASSES_2, BANK_COLS], U8, align_bytes=64)
+        dv_grouped = keep.tile([P, PASSES_2, SAMPLES, PACK], BF16, align_bytes=64)
+        dv_codes = keep.tile([P, PASSES_2, SAMPLES], U32, align_bytes=64)
+        dv_scales = keep.tile([P, PASSES_2, SAMPLES], U8, align_bytes=64)
+        mu = keep.tile([P, SAMPLE_TILES, LINES], BF16)
+
+        def quantise(grouped, n_banks, codes, scales):
+            for bank in range(n_banks):
+                nc.vector.quantize_mx(
+                    out=codes[:, bank, :].bitcast(FP8X4),
+                    scales=scales[:, bank, :],
+                    in_=grouped[:, bank].rearrange("p s r t -> p (s r t)"),
+                )
+
+        def prepare(words, n_banks, codes, scales, chunk_before):
+            grouped = grouped_pool.tile([P, CHUNK_BANKS, 2, P, PACK], BF16, align_bytes=64)
+            for bank in range(n_banks):
+                flipped = bank_pool.tile([P, 2, 2, P], F32, tag="bank")
+                for s in range(2):
+                    for h in range(2):
+                        nc.tensor.transpose(flipped[:, s, h, :], words[:, bank, s, h, :], identity[:])
+                pairs_in = flipped[:].rearrange("p s h r -> p s r h")
+                pairs_out = grouped[:, bank].bitcast(F32)
+                if bank % CHUNK_BANKS == CHUNK_BANKS - 1:
+                    nc.vector.tensor_copy(out=pairs_out, in_=pairs_in)
+                else:
+                    nc.scalar.copy(out=pairs_out, in_=pairs_in)
+            if chunk_before is not None:
+                quantise(*chunk_before)
+            return (grouped, n_banks, codes, scales)
+
+        volt_rows = Volt.rearrange("(s p) k -> p s k", p=P)
+        volt_chunk_k = CHUNK_K // SAMPLE_TILES
+        unquantised = None
+        for c in range(VOLT_CHUNKS):
+            raw = raw_pool.tile([P, SAMPLE_TILES, volt_chunk_k], BF16, tag="raw")
+            nc.sync.dma_start(out=raw[:], in_=volt_rows[:, :, c * volt_chunk_k : (c + 1) * volt_chunk_k])
+            passes = slice(c * CHUNK_BANKS, (c + 1) * CHUNK_BANKS)
+            unquantised = prepare(
+                raw[:].bitcast(F32).rearrange("p s (b h w) -> p b s h w", b=CHUNK_BANKS, h=2),
+                CHUNK_BANKS,
+                volt_codes[:, passes, :],
+                volt_scales[:, passes, :],
+                unquantised,
+            )
+
+        im_rows = IM.rearrange("(g u p e) k -> g u e p k", g=PASSES_2, u=2, p=P, e=2)
+        ybr_rows = Ybr.rearrange("(q s p) l -> q p s l", q=YBR_UNITS, s=2, p=P)
+
+        def first_matmul(g, u, e, acc, im_codes, im_scales):
+            for a in range(PASSES_1):
+                nc.tensor.matmul_mx(
+                    out=acc[:, e, :],
+                    lhsT=im_codes[:, a, :].bitcast(FP8X4),
+                    lhsT_scale=im_scales[:, a, :],
+                    rhs=volt_codes[:, a, :].bitcast(FP8X4),
+                    rhs_scale=volt_scales[:, a, :],
+                    start=(a == 0),
+                    stop=(a == PASSES_1 - 1),
+                )
+            if e == 1:
+                nc.vector.tensor_copy(
+                    out=dv_grouped[:, g, :, 2 * u : 2 * u + 2], in_=acc[:].rearrange("p e b -> p b e")
+                )
+            if e == 1 and u == 1:
+                nc.vector.quantize_mx(
+                    out=dv_codes[:, g, :].bitcast(FP8X4),
+                    scales=dv_scales[:, g, :],
+                    in_=dv_grouped[:, g].rearrange("p b t -> p (b t)"),
+                )
+
+        tile_before = None
+        acc = None
+        for step in range(IM_TILES + 1):
+            if step < IM_TILES:
+                g, u, e = step // 4, (step // 2) % 2, step % 2
+                im_codes = im_pool.tile([P, PASSES_1, P], U32, align_bytes=64)
+                im_scales = im_pool.tile([P, PASSES_1, P], U8, align_bytes=64)
+                for c in range(IM_CHUNKS):
+                    raw = raw_pool.tile([P, CHUNK_K], BF16, tag="raw")
+                    nc.sync.dma_start(out=raw[:], in_=im_rows[g, u, e, :, c * CHUNK_K : (c + 1) * CHUNK_K])
+                    passes = slice(c * 2 * CHUNK_BANKS, (c + 1) * 2 * CHUNK_BANKS)
+                    unquantised = prepare(
+                        raw[:].bitcast(F32).rearrange("p (b s h w) -> p b s h w", b=CHUNK_BANKS, s=2, h=2),
+                        CHUNK_BANKS,
+                        im_codes[:, passes, :].rearrange("p (b s) r -> p b (s r)", s=2),
+                        im_scales[:, passes, :].rearrange("p (b s) r -> p b (s r)", s=2),
+                        unquantised,
+                    )
+                if step == FIRST_YBR_STEP:
+                    nc.sync.dma_start(out=mu[:], in_=n_o_mu_i_u.rearrange("(t p) l -> p t l", p=P))
+                if step >= FIRST_YBR_STEP:
+                    q = step - FIRST_YBR_STEP
+                    raw = raw_pool.tile([P, 2, CURRENTS], BF16, tag="raw")
+                    nc.sync.dma_start(out=raw[:], in_=ybr_rows[q])
+                    unquantised = prepare(
+                        raw[:].bitcast(F32).rearrange("p s (b h w) -> p b s h w", b=PASSES_2, h=2),
+                        PASSES_2,
+                        ybr_codes[:, q],
+                        ybr_scales[:, q],
+                        unquantised,
+                    )
+            else:
+                quantise(*unquantised)
+            if tile_before is not None:
+                if tile_before[2] == 0:
+                    acc = acc_pool.tile([P, 2, SAMPLES], F32, tag="acc")
+                first_matmul(*tile_before[0:3], acc, *tile_before[3:5])
+            if step < IM_TILES:
+                tile_before = (g, u, e, im_codes, im_scales)
+
+        for t in range(SAMPLE_TILES):
+            negative_part = work.tile([P, LINES], F32)
+            nc.scalar.activation(
+                out=negative_part[:], in_=mu[:, t, :], func=ACT.Relu, scale=-1.0,
+                accum_out=terms[:, t, 0, LINE_TILES : LINE_TILES + 1],
+            )
+
+        for t in range(SAMPLE_TILES):
+            samples = slice(t * P, (t + 1) * P)
+            for q in range(LINE_TILES):
+                ibr = bank_pool.tile([P, 2, BANK_COLS], F32, tag="bank")
+                for part in range(2):
+                    for g in range(PASSES_2):
+                        nc.tensor.matmul_mx(
+                            out=ibr[:, part, :],
+                            lhsT=dv_codes[:, g, samples].bitcast(FP8X4),
+                            lhsT_scale=dv_scales[:, g, samples],
+                            rhs=ybr_codes[:, part * LINE_TILES + q, g, :].bitcast(FP8X4),
+                            rhs_scale=ybr_scales[:, part * LINE_TILES + q, g, :],
+                            start=(g == 0),
+                            stop=(g == PASSES_2 - 1),
+                        )
+                squares = work.tile([P, 2, BANK_COLS], F32)
+                nc.scalar.activation(out=squares[:], in_=ibr[:], func=ACT.Square)
+                i_up = work.tile([P, BANK_COLS], F32)
+                nc.vector.scalar_tensor_tensor(
+                    out=i_up[:], in0=squares[:, 0, :], scalar=-LIMIT_SQUARED, in1=squares[:, 1, :],
+                    op0=ALU.add, op1=ALU.add,
+                )
+                excess = work.tile([P, BANK_COLS], F32)
+                nc.vector.tensor_scalar(
+                    out=excess[:], in0=i_up[:], scalar1=0.0, scalar2=None, op0=ALU.max, op1=ALU.add,
+                    accum_out=terms[:, t, 1, q : q + 1],
+                )
+                slack = work.tile([P, BANK_COLS], F32)
+                nc.vector.tensor_tensor(
+                    out=slack[:], in0=i_up[:], in1=mu[:, t, q * BANK_COLS : (q + 1) * BANK_COLS], op=ALU.mult
+                )
+                slack_size = work.tile([P, BANK_COLS], F32)
+                nc.scalar.activation(
+                    out=slack_size[:], in_=slack[:], func=ACT.Abs, accum_out=terms[:, t, 0, q : q + 1]
+                )
+
+        nc.vector.tensor_reduce(
+            out=totals[:, 0:SAMPLE_TILES], in_=terms[:].rearrange("p t w c -> p t (w c)"),
+            axis=mybir.AxisListType.X, op=ALU.add,
+        )
+        totals_flipped = acc_pool.tile([P, P], F32, tag="acc")
+        nc.tensor.transpose(totals_flipped[:], totals[:], identity[:])
+        rows = keep.tile([P, P], F32)
+        nc.vector.tensor_copy(out=rows[:], in_=totals_flipped[:])
+        nc.sync.dma_start(out=out.rearrange("(t b) -> t b", t=SAMPLE_TILES), in_=rows[0:SAMPLE_TILES, :])

@@ -32,7 +32,7 @@ IM_TILES = CURRENTS // P
 IM_CHUNKS = VOLTS // CHUNK_K
 VOLT_CHUNKS = SAMPLES * VOLTS // (P * CHUNK_K)
 YBR_UNITS = CURRENTS // BANK_COLS
-FIRST_YBR_STEP = IM_TILES - YBR_UNITS
+FIRST_YBR_TILE = IM_TILES - YBR_UNITS
 LINE_TILES = LINES // BANK_COLS
 
 FLOPS = 2 * SAMPLES * CURRENTS * (VOLTS + CURRENTS)
@@ -86,7 +86,7 @@ def tile_pinnlayer_pa_k_kernel(tc, Volt, IM, Ybr, n_o_mu_i_u, out):
                         nc.tensor.transpose(flipped[:, s, h, :], words[:, bank, s, h, :], identity[:])
                 pairs_in = flipped[:].rearrange("p s h r -> p s r h")
                 pairs_out = grouped[:, bank].bitcast(F32)
-                if bank % CHUNK_BANKS == CHUNK_BANKS - 1:
+                if bank == n_banks - 1:
                     nc.vector.tensor_copy(out=pairs_out, in_=pairs_in)
                 else:
                     nc.scalar.copy(out=pairs_out, in_=pairs_in)
@@ -112,8 +112,8 @@ def tile_pinnlayer_pa_k_kernel(tc, Volt, IM, Ybr, n_o_mu_i_u, out):
         im_rows = IM.rearrange("(g u p e) k -> g u e p k", g=PASSES_2, u=2, p=P, e=2)
         ybr_rows = Ybr.rearrange("(q s p) l -> q p s l", q=YBR_UNITS, s=2, p=P)
 
-        def first_matmul(g, u, e, acc, im_codes, im_scales):
-            for a in range(PASSES_1):
+        def first_matmul(g, u, e, acc, im_codes, im_scales, passes):
+            for a in passes:
                 nc.tensor.matmul_mx(
                     out=acc[:, e, :],
                     lhsT=im_codes[:, a, :].bitcast(FP8X4),
@@ -123,28 +123,32 @@ def tile_pinnlayer_pa_k_kernel(tc, Volt, IM, Ybr, n_o_mu_i_u, out):
                     start=(a == 0),
                     stop=(a == PASSES_1 - 1),
                 )
-            if e == 1:
+            if a == PASSES_1 - 1 and e == 1:
                 nc.vector.tensor_copy(
                     out=dv_grouped[:, g, :, 2 * u : 2 * u + 2], in_=acc[:].rearrange("p e b -> p b e")
                 )
-            if e == 1 and u == 1:
+            if a == PASSES_1 - 1 and e == 1 and u == 1:
                 nc.vector.quantize_mx(
                     out=dv_codes[:, g, :].bitcast(FP8X4),
                     scales=dv_scales[:, g, :],
                     in_=dv_grouped[:, g].rearrange("p b t -> p (b t)"),
                 )
 
+        chunk_passes = PASSES_1 // IM_CHUNKS
         tile_before = None
-        acc = None
-        for step in range(IM_TILES + 1):
-            if step < IM_TILES:
-                g, u, e = step // 4, (step // 2) % 2, step % 2
+        for j in range(IM_TILES + 1):
+            if j < IM_TILES:
+                g, u, e = j // 4, (j // 2) % 2, j % 2
                 im_codes = im_pool.tile([P, PASSES_1, P], U32, align_bytes=64)
                 im_scales = im_pool.tile([P, PASSES_1, P], U8, align_bytes=64)
-                for c in range(IM_CHUNKS):
+                if e == 0:
+                    acc = acc_pool.tile([P, 2, SAMPLES], F32, tag="acc")
+            for c in range(IM_CHUNKS):
+                first = c * chunk_passes
+                if j < IM_TILES:
                     raw = raw_pool.tile([P, CHUNK_K], BF16, tag="raw")
                     nc.sync.dma_start(out=raw[:], in_=im_rows[g, u, e, :, c * CHUNK_K : (c + 1) * CHUNK_K])
-                    passes = slice(c * 2 * CHUNK_BANKS, (c + 1) * 2 * CHUNK_BANKS)
+                    passes = slice(first, first + chunk_passes)
                     unquantised = prepare(
                         raw[:].bitcast(F32).rearrange("p (b s h w) -> p b s h w", b=CHUNK_BANKS, s=2, h=2),
                         CHUNK_BANKS,
@@ -152,10 +156,12 @@ def tile_pinnlayer_pa_k_kernel(tc, Volt, IM, Ybr, n_o_mu_i_u, out):
                         im_scales[:, passes, :].rearrange("p (b s) r -> p b (s r)", s=2),
                         unquantised,
                     )
-                if step == FIRST_YBR_STEP:
-                    nc.sync.dma_start(out=mu[:], in_=n_o_mu_i_u.rearrange("(t p) l -> p t l", p=P))
-                if step >= FIRST_YBR_STEP:
-                    q = step - FIRST_YBR_STEP
+                elif c == 0:
+                    quantise(*unquantised)
+                if tile_before is not None:
+                    first_matmul(*tile_before, range(first, first + chunk_passes // 2))
+                if FIRST_YBR_TILE <= j < IM_TILES and c == IM_CHUNKS - 1:
+                    q = j - FIRST_YBR_TILE
                     raw = raw_pool.tile([P, 2, CURRENTS], BF16, tag="raw")
                     nc.sync.dma_start(out=raw[:], in_=ybr_rows[q])
                     unquantised = prepare(
@@ -165,14 +171,11 @@ def tile_pinnlayer_pa_k_kernel(tc, Volt, IM, Ybr, n_o_mu_i_u, out):
                         ybr_scales[:, q],
                         unquantised,
                     )
-            else:
-                quantise(*unquantised)
-            if tile_before is not None:
-                if tile_before[2] == 0:
-                    acc = acc_pool.tile([P, 2, SAMPLES], F32, tag="acc")
-                first_matmul(*tile_before[0:3], acc, *tile_before[3:5])
-            if step < IM_TILES:
-                tile_before = (g, u, e, im_codes, im_scales)
+                if tile_before is not None:
+                    first_matmul(*tile_before, range(first + chunk_passes // 2, first + chunk_passes))
+            if j < IM_TILES:
+                tile_before = (g, u, e, acc, im_codes, im_scales)
+        nc.sync.dma_start(out=mu[:], in_=n_o_mu_i_u.rearrange("(t p) l -> p t l", p=P))
 
         for t in range(SAMPLE_TILES):
             negative_part = work.tile([P, LINES], F32)

@@ -32,7 +32,7 @@ IM_TILES = CURRENTS // P
 IM_CHUNKS = VOLTS // CHUNK_K
 VOLT_CHUNKS = SAMPLES * VOLTS // (P * CHUNK_K)
 YBR_UNITS = CURRENTS // BANK_COLS
-FIRST_YBR_TILE = IM_TILES - YBR_UNITS
+FIRST_YBR_STEP = IM_TILES + 1 - YBR_UNITS
 LINE_TILES = LINES // BANK_COLS
 
 FLOPS = 2 * SAMPLES * CURRENTS * (VOLTS + CURRENTS)
@@ -112,8 +112,8 @@ def tile_pinnlayer_pa_k_kernel(tc, Volt, IM, Ybr, n_o_mu_i_u, out):
         im_rows = IM.rearrange("(g u p e) k -> g u e p k", g=PASSES_2, u=2, p=P, e=2)
         ybr_rows = Ybr.rearrange("(q s p) l -> q p s l", q=YBR_UNITS, s=2, p=P)
 
-        def first_matmul(g, u, e, acc, im_codes, im_scales, passes):
-            for a in passes:
+        def first_matmul(g, u, e, acc, im_codes, im_scales):
+            for a in range(PASSES_1):
                 nc.tensor.matmul_mx(
                     out=acc[:, e, :],
                     lhsT=im_codes[:, a, :].bitcast(FP8X4),
@@ -123,32 +123,28 @@ def tile_pinnlayer_pa_k_kernel(tc, Volt, IM, Ybr, n_o_mu_i_u, out):
                     start=(a == 0),
                     stop=(a == PASSES_1 - 1),
                 )
-            if a == PASSES_1 - 1 and e == 1:
+            if e == 1:
                 nc.vector.tensor_copy(
                     out=dv_grouped[:, g, :, 2 * u : 2 * u + 2], in_=acc[:].rearrange("p e b -> p b e")
                 )
-            if a == PASSES_1 - 1 and e == 1 and u == 1:
+            if e == 1 and u == 1:
                 nc.vector.quantize_mx(
                     out=dv_codes[:, g, :].bitcast(FP8X4),
                     scales=dv_scales[:, g, :],
                     in_=dv_grouped[:, g].rearrange("p b t -> p (b t)"),
                 )
 
-        chunk_passes = PASSES_1 // IM_CHUNKS
         tile_before = None
-        for j in range(IM_TILES + 1):
-            if j < IM_TILES:
-                g, u, e = j // 4, (j // 2) % 2, j % 2
+        acc = None
+        for step in range(IM_TILES + 1):
+            if step < IM_TILES:
+                g, u, e = step // 4, (step // 2) % 2, step % 2
                 im_codes = im_pool.tile([P, PASSES_1, P], U32, align_bytes=64)
                 im_scales = im_pool.tile([P, PASSES_1, P], U8, align_bytes=64)
-                if e == 0:
-                    acc = acc_pool.tile([P, 2, SAMPLES], F32, tag="acc")
-            for c in range(IM_CHUNKS):
-                first = c * chunk_passes
-                if j < IM_TILES:
+                for c in range(IM_CHUNKS):
                     raw = raw_pool.tile([P, CHUNK_K], BF16, tag="raw")
                     nc.sync.dma_start(out=raw[:], in_=im_rows[g, u, e, :, c * CHUNK_K : (c + 1) * CHUNK_K])
-                    passes = slice(first, first + chunk_passes)
+                    passes = slice(c * 2 * CHUNK_BANKS, (c + 1) * 2 * CHUNK_BANKS)
                     unquantised = prepare(
                         raw[:].bitcast(F32).rearrange("p (b s h w) -> p b s h w", b=CHUNK_BANKS, s=2, h=2),
                         CHUNK_BANKS,
@@ -156,37 +152,46 @@ def tile_pinnlayer_pa_k_kernel(tc, Volt, IM, Ybr, n_o_mu_i_u, out):
                         im_scales[:, passes, :].rearrange("p (b s) r -> p b (s r)", s=2),
                         unquantised,
                     )
-                elif c == 0:
-                    quantise(*unquantised)
-                if tile_before is not None:
-                    first_matmul(*tile_before, range(first, first + chunk_passes // 2))
-                if FIRST_YBR_TILE <= j < IM_TILES and c == IM_CHUNKS - 1:
-                    q = j - FIRST_YBR_TILE
-                    raw = raw_pool.tile([P, 2, CURRENTS], BF16, tag="raw")
-                    nc.sync.dma_start(out=raw[:], in_=ybr_rows[q])
-                    unquantised = prepare(
-                        raw[:].bitcast(F32).rearrange("p s (b h w) -> p b s h w", b=PASSES_2, h=2),
-                        PASSES_2,
-                        ybr_codes[:, q],
-                        ybr_scales[:, q],
-                        unquantised,
+            else:
+                quantise(*unquantised)
+                unquantised = None
+                for t in range(SAMPLE_TILES):
+                    negative_part = work.tile([P, LINES], F32)
+                    nc.scalar.activation(
+                        out=negative_part[:], in_=mu[:, t, :], func=ACT.Relu, scale=-1.0,
+                        accum_out=terms[:, t, 0, LINE_TILES : LINE_TILES + 1],
                     )
-                if tile_before is not None:
-                    first_matmul(*tile_before, range(first + chunk_passes // 2, first + chunk_passes))
-            if j < IM_TILES:
-                tile_before = (g, u, e, acc, im_codes, im_scales)
-        nc.sync.dma_start(out=mu[:], in_=n_o_mu_i_u.rearrange("(t p) l -> p t l", p=P))
+            if tile_before is not None:
+                if tile_before[2] == 0:
+                    acc = acc_pool.tile([P, 2, SAMPLES], F32, tag="acc")
+                first_matmul(*tile_before[0:3], acc, *tile_before[3:5])
+            if step < IM_TILES:
+                tile_before = (g, u, e, im_codes, im_scales)
+            if step == FIRST_YBR_STEP:
+                nc.sync.dma_start(out=mu[:], in_=n_o_mu_i_u.rearrange("(t p) l -> p t l", p=P))
+            if step >= FIRST_YBR_STEP:
+                unit = step - FIRST_YBR_STEP
+                raw = raw_pool.tile([P, 2, CURRENTS], BF16, tag="raw")
+                nc.sync.dma_start(out=raw[:], in_=ybr_rows[unit])
+                unquantised = prepare(
+                    raw[:].bitcast(F32).rearrange("p s (b h w) -> p b s h w", b=PASSES_2, h=2),
+                    PASSES_2,
+                    ybr_codes[:, unit],
+                    ybr_scales[:, unit],
+                    unquantised,
+                )
+        quantise(*unquantised)
 
-        for t in range(SAMPLE_TILES):
-            negative_part = work.tile([P, LINES], F32)
+        def sum_of_sizes(t, q, slack):
+            slack_size = work.tile([P, BANK_COLS], F32)
             nc.scalar.activation(
-                out=negative_part[:], in_=mu[:, t, :], func=ACT.Relu, scale=-1.0,
-                accum_out=terms[:, t, 0, LINE_TILES : LINE_TILES + 1],
+                out=slack_size[:], in_=slack[:], func=ACT.Abs, accum_out=terms[:, t, 0, q : q + 1]
             )
 
-        for t in range(SAMPLE_TILES):
-            samples = slice(t * P, (t + 1) * P)
-            for q in range(LINE_TILES):
+        bank_before = None
+        for q in range(LINE_TILES):
+            for t in range(SAMPLE_TILES):
+                samples = slice(t * P, (t + 1) * P)
                 ibr = bank_pool.tile([P, 2, BANK_COLS], F32, tag="bank")
                 for part in range(2):
                     for g in range(PASSES_2):
@@ -206,19 +211,19 @@ def tile_pinnlayer_pa_k_kernel(tc, Volt, IM, Ybr, n_o_mu_i_u, out):
                     out=i_up[:], in0=squares[:, 0, :], scalar=-LIMIT_SQUARED, in1=squares[:, 1, :],
                     op0=ALU.add, op1=ALU.add,
                 )
+                slack = work.tile([P, BANK_COLS], F32)
+                nc.vector.tensor_tensor(
+                    out=slack[:], in0=i_up[:], in1=mu[:, t, q * BANK_COLS : (q + 1) * BANK_COLS], op=ALU.mult
+                )
                 excess = work.tile([P, BANK_COLS], F32)
                 nc.vector.tensor_scalar(
                     out=excess[:], in0=i_up[:], scalar1=0.0, scalar2=None, op0=ALU.max, op1=ALU.add,
                     accum_out=terms[:, t, 1, q : q + 1],
                 )
-                slack = work.tile([P, BANK_COLS], F32)
-                nc.vector.tensor_tensor(
-                    out=slack[:], in0=i_up[:], in1=mu[:, t, q * BANK_COLS : (q + 1) * BANK_COLS], op=ALU.mult
-                )
-                slack_size = work.tile([P, BANK_COLS], F32)
-                nc.scalar.activation(
-                    out=slack_size[:], in_=slack[:], func=ACT.Abs, accum_out=terms[:, t, 0, q : q + 1]
-                )
+                if bank_before is not None:
+                    sum_of_sizes(*bank_before)
+                bank_before = (t, q, slack)
+        sum_of_sizes(*bank_before)
 
         nc.vector.tensor_reduce(
             out=totals[:, 0:SAMPLE_TILES], in_=terms[:].rearrange("p t w c -> p t (w c)"),

from contextlib import ExitStack

import concourse.mybir as mybir
from concourse.masks import make_identity

F32 = mybir.dt.float32
BF16 = mybir.dt.bfloat16
U32 = mybir.dt.uint32
U8 = mybir.dt.uint8
FP8X4 = mybir.dt.float8_e4m3fn_x4
ALU = mybir.AluOpType
ACT = mybir.ActivationFunctionType

P = 128
PACK = 4
K_PASS = P * PACK

SAMPLES = 256
VOLTS = 8192
CURRENTS = 1536
LINES = CURRENTS // 2
LIMIT_SQUARED = 1.0

PASSES_1 = VOLTS // K_PASS
PASSES_2 = CURRENTS // K_PASS
SAMPLE_TILES = SAMPLES // P

BANK_COLS = 2 * P
CHUNK_BANKS = 4
CHUNK_K = 4096
IM_TILES = CURRENTS // P
IM_CHUNKS = VOLTS // CHUNK_K
VOLT_CHUNKS = SAMPLES * VOLTS // (P * CHUNK_K)
YBR_UNITS = CURRENTS // BANK_COLS
FIRST_YBR_STEP = IM_TILES + 1 - YBR_UNITS
LINE_TILES = LINES // BANK_COLS

FLOPS = 2 * SAMPLES * CURRENTS * (VOLTS + CURRENTS)


def tile_pinnlayer_pa_k_kernel(tc, Volt, IM, Ybr, n_o_mu_i_u, out):
    nc = tc.nc
    with ExitStack() as ctx:
        keep = ctx.enter_context(tc.tile_pool(name="keep", bufs=1))
        raw_pool = ctx.enter_context(tc.tile_pool(name="raw", bufs=8))
        grouped_pool = ctx.enter_context(tc.tile_pool(name="grouped", bufs=3))
        im_pool = ctx.enter_context(tc.tile_pool(name="im", bufs=3))
        work = ctx.enter_context(tc.tile_pool(name="work", bufs=3))
        bank_pool = ctx.enter_context(tc.psum_pool(name="bank", bufs=6))
        acc_pool = ctx.enter_context(tc.psum_pool(name="acc", bufs=2))
        ctx.enter_context(tc.manual_schedule())

        identity = keep.tile([P, P], F32)
        make_identity(nc, identity[:])

        terms = keep.tile([P, SAMPLE_TILES, 2, 8], F32)
        nc.vector.memset(terms[:], 0.0)
        totals = keep.tile([P, P], F32)
        nc.vector.memset(totals[:], 0.0)
        table_warmer = keep.tile([P, 1], F32)
        nc.scalar.activation(out=table_warmer[:], in_=totals[:, 0:1], func=ACT.Abs)

        volt_codes = keep.tile([P, PASSES_1, SAMPLES], U32, align_bytes=64)
        volt_scales = keep.tile([P, PASSES_1, SAMPLES], U8, align_bytes=64)
        ybr_codes = keep.tile([P, YBR_UNITS, PASSES_2, BANK_COLS], U32, align_bytes=64)
        ybr_scales = keep.tile([P, YBR_UNITS, PASSES_2, BANK_COLS], U8, align_bytes=64)
        dv_grouped = keep.tile([P, PASSES_2, SAMPLES, PACK], BF16, align_bytes=64)
        dv_codes = keep.tile([P, PASSES_2, SAMPLES], U32, align_bytes=64)
        dv_scales = keep.tile([P, PASSES_2, SAMPLES], U8, align_bytes=64)
        mu = keep.tile([P, SAMPLE_TILES, LINES], BF16)

        def quantise(grouped, n_banks, codes, scales):
            for bank in range(n_banks):
                nc.vector.quantize_mx(
                    out=codes[:, bank, :].bitcast(FP8X4),
                    scales=scales[:, bank, :],
                    in_=grouped[:, bank].rearrange("p s r t -> p (s r t)"),
                )

        def prepare(words, n_banks, codes, scales, chunk_before):
            grouped = grouped_pool.tile([P, CHUNK_BANKS, 2, P, PACK], BF16, align_bytes=64)
            for bank in range(n_banks):
                flipped = bank_pool.tile([P, 2, 2, P], F32, tag="bank")
                for s in range(2):
                    for h in range(2):
                        nc.tensor.transpose(flipped[:, s, h, :], words[:, bank, s, h, :], identity[:])
                pairs_in = flipped[:].rearrange("p s h r -> p s r h")
                pairs_out = grouped[:, bank].bitcast(F32)
                if bank == n_banks - 1:
                    nc.vector.tensor_copy(out=pairs_out, in_=pairs_in)
                else:
                    nc.scalar.copy(out=pairs_out, in_=pairs_in)
            if chunk_before is not None:
                quantise(*chunk_before)
            return (grouped, n_banks, codes, scales)

        volt_rows = Volt.rearrange("(s p) k -> p s k", p=P)
        volt_chunk_k = CHUNK_K // SAMPLE_TILES
        unquantised = None
        for c in range(VOLT_CHUNKS):
            raw = raw_pool.tile([P, SAMPLE_TILES, volt_chunk_k], BF16, tag="raw")
            nc.sync.dma_start(out=raw[:], in_=volt_rows[:, :, c * volt_chunk_k : (c + 1) * volt_chunk_k])
            passes = slice(c * CHUNK_BANKS, (c + 1) * CHUNK_BANKS)
            unquantised = prepare(
                raw[:].bitcast(F32).rearrange("p s (b h w) -> p b s h w", b=CHUNK_BANKS, h=2),
                CHUNK_BANKS,
                volt_codes[:, passes, :],
                volt_scales[:, passes, :],
                unquantised,
            )

        im_rows = IM.rearrange("(g u p e) k -> g u e p k", g=PASSES_2, u=2, p=P, e=2)
        ybr_rows = Ybr.rearrange("(q s p) l -> q p s l", q=YBR_UNITS, s=2, p=P)

        def first_matmul(g, u, e, acc, im_codes, im_scales):
            for a in range(PASSES_1):
                nc.tensor.matmul_mx(
                    out=acc[:, e, :],
                    lhsT=im_codes[:, a, :].bitcast(FP8X4),
                    lhsT_scale=im_scales[:, a, :],
                    rhs=volt_codes[:, a, :].bitcast(FP8X4),
                    rhs_scale=volt_scales[:, a, :],
                    start=(a == 0),
                    stop=(a == PASSES_1 - 1),
                )
            if e == 1:
                nc.vector.tensor_copy(
                    out=dv_grouped[:, g, :, 2 * u : 2 * u + 2], in_=acc[:].rearrange("p e b -> p b e")
                )
            if e == 1 and u == 1:
                nc.vector.quantize_mx(
                    out=dv_codes[:, g, :].bitcast(FP8X4),
                    scales=dv_scales[:, g, :],
                    in_=dv_grouped[:, g].rearrange("p b t -> p (b t)"),
                )

        tile_before = None
        acc = None
        for step in range(IM_TILES + 1):
            if step < IM_TILES:
                g, u, e = step // 4, (step // 2) % 2, step % 2
                im_codes = im_pool.tile([P, PASSES_1, P], U32, align_bytes=64)
                im_scales = im_pool.tile([P, PASSES_1, P], U8, align_bytes=64)
                for c in range(IM_CHUNKS):
                    raw = raw_pool.tile([P, CHUNK_K], BF16, tag="raw")
                    nc.sync.dma_start(out=raw[:], in_=im_rows[g, u, e, :, c * CHUNK_K : (c + 1) * CHUNK_K])
                    passes = slice(c * 2 * CHUNK_BANKS, (c + 1) * 2 * CHUNK_BANKS)
                    unquantised = prepare(
                        raw[:].bitcast(F32).rearrange("p (b s h w) -> p b s h w", b=CHUNK_BANKS, s=2, h=2),
                        CHUNK_BANKS,
                        im_codes[:, passes, :].rearrange("p (b s) r -> p b (s r)", s=2),
                        im_scales[:, passes, :].rearrange("p (b s) r -> p b (s r)", s=2),
                        unquantised,
                    )
            else:
                quantise(*unquantised)
                unquantised = None
                for t in range(SAMPLE_TILES):
                    negative_part = work.tile([P, LINES], F32)
                    nc.scalar.activation(
                        out=negative_part[:], in_=mu[:, t, :], func=ACT.Relu, scale=-1.0,
                        accum_out=terms[:, t, 0, LINE_TILES : LINE_TILES + 1],
                    )
            if tile_before is not None:
                if tile_before[2] == 0:
                    acc = acc_pool.tile([P, 2, SAMPLES], F32, tag="acc")
                first_matmul(*tile_before[0:3], acc, *tile_before[3:5])
            if step < IM_TILES:
                tile_before = (g, u, e, im_codes, im_scales)
            if step == FIRST_YBR_STEP:
                nc.sync.dma_start(out=mu[:], in_=n_o_mu_i_u.rearrange("(t p) l -> p t l", p=P))
            if step >= FIRST_YBR_STEP:
                unit = step - FIRST_YBR_STEP
                raw = raw_pool.tile([P, 2, CURRENTS], BF16, tag="raw")
                nc.sync.dma_start(out=raw[:], in_=ybr_rows[unit])
                unquantised = prepare(
                    raw[:].bitcast(F32).rearrange("p s (b h w) -> p b s h w", b=PASSES_2, h=2),
                    PASSES_2,
                    ybr_codes[:, unit],
                    ybr_scales[:, unit],
                    unquantised,
                )
        quantise(*unquantised)

        def sum_of_sizes(t, q, slack):
            slack_size = work.tile([P, BANK_COLS], F32)
            nc.scalar.activation(
                out=slack_size[:], in_=slack[:], func=ACT.Abs, accum_out=terms[:, t, 0, q : q + 1]
            )

        bank_before = None
        for q in range(LINE_TILES):
            for t in range(SAMPLE_TILES):
                samples = slice(t * P, (t + 1) * P)
                ibr = bank_pool.tile([P, 2, BANK_COLS], F32, tag="bank")
                for part in range(2):
                    for g in range(PASSES_2):
                        nc.tensor.matmul_mx(
                            out=ibr[:, part, :],
                            lhsT=dv_codes[:, g, samples].bitcast(FP8X4),
                            lhsT_scale=dv_scales[:, g, samples],
                            rhs=ybr_codes[:, part * LINE_TILES + q, g, :].bitcast(FP8X4),
                            rhs_scale=ybr_scales[:, part * LINE_TILES + q, g, :],
                            start=(g == 0),
                            stop=(g == PASSES_2 - 1),
                        )
                squares = work.tile([P, 2, BANK_COLS], F32)
                nc.scalar.activation(out=squares[:], in_=ibr[:], func=ACT.Square)
                i_up = work.tile([P, BANK_COLS], F32)
                nc.vector.scalar_tensor_tensor(
                    out=i_up[:], in0=squares[:, 0, :], scalar=-LIMIT_SQUARED, in1=squares[:, 1, :],
                    op0=ALU.add, op1=ALU.add,
                )
                slack = work.tile([P, BANK_COLS], F32)
                nc.vector.tensor_tensor(
                    out=slack[:], in0=i_up[:], in1=mu[:, t, q * BANK_COLS : (q + 1) * BANK_COLS], op=ALU.mult
                )
                excess = work.tile([P, BANK_COLS], F32)
                nc.vector.tensor_scalar(
                    out=excess[:], in0=i_up[:], scalar1=0.0, scalar2=None, op0=ALU.max, op1=ALU.add,
                    accum_out=terms[:, t, 1, q : q + 1],
                )
                if bank_before is not None:
                    sum_of_sizes(*bank_before)
                bank_before = (t, q, slack)
        sum_of_sizes(*bank_before)

        nc.vector.tensor_reduce(
            out=totals[:, 0:SAMPLE_TILES], in_=terms[:].rearrange("p t w c -> p t (w c)"),
            axis=mybir.AxisListType.X, op=ALU.add,
        )
        totals_flipped = acc_pool.tile([P, P], F32, tag="acc")
        nc.tensor.transpose(totals_flipped[:], totals[:], identity[:])
        rows = keep.tile([P, P], F32)
        nc.vector.tensor_copy(out=rows[:], in_=totals_flipped[:])
        nc.sync.dma_start(out=out.rearrange("(t b) -> t b", t=SAMPLE_TILES), in_=rows[0:SAMPLE_TILES, :])
